import numpy as np
import ml_dtypes


BF16 = ml_dtypes.bfloat16


def bf(x):
    return np.asarray(x, np.float32).astype(BF16)


def f64(x):
    return np.asarray(x).astype(np.float64)


E2M1 = np.array([0.0, 0.5, 1.0, 1.5, 2.0, 3.0, 4.0, 6.0, -0.0, -0.5, -1.0, -1.5, -2.0, -3.0, -4.0, -6.0])


def pack_weight(w, fmt):
    k, n = w.shape
    w = f64(bf(w)).reshape(k // 32, 32, n)
    amax = np.abs(w).max(1)
    if fmt == "e4m3":
        byte = np.frexp(amax)[1] - 1 + 127 - 7
    else:
        mant, ex = np.frexp(amax / 6.0)
        byte = np.where(mant > 0.5, ex, ex - 1) + 127
    byte = np.clip(np.where(amax > 0, byte, 1), 1, 254)
    scaled = (w * np.exp2(127.0 - byte)[:, None, :]).reshape(k, n).astype(np.float32)
    by_word = np.ascontiguousarray(scaled.reshape(k // 512, 128, 4, n).transpose(0, 1, 3, 2))
    if fmt == "e4m3":
        words = by_word.astype(ml_dtypes.float8_e4m3fn).view(np.uint8)
    else:
        c = by_word.astype(ml_dtypes.float4_e2m1fn).view(np.uint8) & 0xF
        words = c[..., 0::2] | (c[..., 1::2] << 4)
    return np.ascontiguousarray(words), np.ascontiguousarray(byte.astype(np.uint8).reshape(k // 512, 16, n))


def unpack_weight(words, scales, fmt):
    g, p, n, _ = words.shape
    if fmt == "e4m3":
        vals = np.ascontiguousarray(words).view(ml_dtypes.float8_e4m3fn).astype(np.float64)
    else:
        nib = np.empty((g, p, n, 4), np.uint8)
        nib[..., 0::2] = words & 0xF
        nib[..., 1::2] = words >> 4
        vals = E2M1[nib]
    vals = vals * np.repeat(np.exp2(scales.astype(np.float64) - 127.0), 8, axis=1)[..., None]
    return vals.transpose(0, 1, 3, 2).reshape(g * 512, n)

def pack4(w):
    words, scales = pack_weight(w, "e2m1")
    return words.reshape(words.shape[0], 128, -1), scales


def unpack4(words, scales):
    return unpack_weight(words.reshape(words.shape[0], 128, -1, 2), scales, "e2m1")


def kspread(k):
    return np.exp2(np.repeat(np.random.randint(-6, 7, k // 32), 32).astype(np.float64))


B, S, D, H, DH = 1, 512, 3072, 16, 96
E = H * DH
HALF = DH // 2
ROPE_BASE = 10000.0


def apply_rope(u):
    inv_freq = 1.0 / ROPE_BASE ** (np.arange(0, DH, 2) / DH)
    freqs = np.arange(S)[:, None] * inv_freq[None, :]
    cos = np.concatenate([np.cos(freqs), np.cos(freqs)], axis=-1)
    sin = np.concatenate([np.sin(freqs), np.sin(freqs)], axis=-1)
    rot = np.concatenate([-u[..., HALF:], u[..., :HALF]], axis=-1)
    return u * cos + rot * sin


def setup_inputs():
    s = kspread(D)
    x = np.random.standard_normal((B, S, D)) * s
    wq = np.random.standard_normal((E, D)) * 0.7 / np.sqrt(D) / s[None, :]
    wk = np.random.standard_normal((E, D)) * 0.7 / np.sqrt(D) / s[None, :]
    x_words, x_scales = pack4(np.ascontiguousarray(x.reshape(B * S, D).T))
    Wq_words, Wq_scales = pack4(np.ascontiguousarray(wq.T))
    Wk_words, Wk_scales = pack4(np.ascontiguousarray(wk.T))
    return {"x_words": x_words, "x_scales": x_scales,
            "Wq_words": Wq_words, "Wq_scales": Wq_scales,
            "Wk_words": Wk_words, "Wk_scales": Wk_scales}


def reference(x_words, x_scales, Wq_words, Wq_scales, Wk_words, Wk_scales):
    xq = unpack4(x_words, x_scales).T.reshape(B, S, D)
    q = (xq @ unpack4(Wq_words, Wq_scales)).reshape(B, S, H, DH).transpose(0, 2, 1, 3)
    k = (xq @ unpack4(Wk_words, Wk_scales)).reshape(B, S, H, DH).transpose(0, 2, 1, 3)
    return apply_rope(q), apply_rope(k)

@@ -1,0 +1,188 @@
+import math
+from contextlib import ExitStack
+
+import concourse.mybir as mybir
+
+F32 = mybir.dt.float32
+I32 = mybir.dt.int32
+U8 = mybir.dt.uint8
+FP4X4 = mybir.dt.float4_e2m1fn_x4
+ADD = mybir.AluOpType.add
+SUB = mybir.AluOpType.subtract
+MULT = mybir.AluOpType.mult
+SIN = mybir.ActivationFunctionType.Sin
+
+P = 128
+TOKENS = 512
+FEATURES = 3072
+OUT_FEATURES = 1536
+HEADS = 16
+HEAD = 96
+HALF = HEAD // 2
+PASSES = FEATURES // 512
+TILES = TOKENS // P
+BLOCK = 512
+BLOCKS = OUT_FEATURES // BLOCK
+ROPE_BASE = 10000.0
+PERIODS = 6
+FLOPS = 2 * TOKENS * FEATURES * 2 * OUT_FEATURES
+
+
+def tile_multiheadattention_pa_kernel(
+    tc, x_words, x_scales, Wq_words, Wq_scales, Wk_words, Wk_scales, out_0, out_1
+):
+    nc = tc.nc
+    with ExitStack() as ctx:
+        ctx.enter_context(tc.manual_schedule())
+        keep = ctx.enter_context(tc.tile_pool(name="keep", bufs=1))
+        prod = ctx.enter_context(tc.tile_pool(name="prod", bufs=8))
+        res = ctx.enter_context(tc.tile_pool(name="res", bufs=6))
+        psum = ctx.enter_context(tc.psum_pool(name="psum", bufs=8))
+
+        x_codes = keep.tile([P, PASSES, 2 * TOKENS], U8, align_bytes=64)
+        x_plane = keep.tile([P, PASSES, TOKENS], U8, align_bytes=64)
+        qa_codes = keep.tile([P, PASSES, 2 * BLOCK], U8, align_bytes=64)
+        qa_plane = keep.tile([P, PASSES, BLOCK], U8, align_bytes=64)
+        qb_codes = keep.tile([P, PASSES, 4 * BLOCK], U8, align_bytes=64)
+        qb_plane = keep.tile([P, PASSES, 2 * BLOCK], U8, align_bytes=64)
+        k_codes = keep.tile([P, PASSES, 6 * BLOCK], U8, align_bytes=64)
+        k_plane = keep.tile([P, PASSES, 3 * BLOCK], U8, align_bytes=64)
+
+        def zero(engine, plane):
+            engine.memset(plane[:].rearrange("p g n -> p (g n)").bitcast(I32), 0)
+
+        def load_codes(tile, words, g0, g1, c0, c1):
+            nc.sync.dma_start(
+                out=tile[:, g0:g1, :].bitcast(I32),
+                in_=words[g0:g1, :, 2 * c0 : 2 * c1].rearrange("g p n -> p g n").bitcast(I32),
+            )
+
+        def load_scales(plane, scales, c0, c1):
+            for q in range(4):
+                nc.sync.dma_start(
+                    out=plane[32 * q : 32 * q + 4, :, :].bitcast(I32),
+                    in_=scales[:, 4 * q : 4 * q + 4, c0:c1].rearrange("g r n -> r g n").bitcast(I32),
+                )
+
+        pos = keep.tile([P, TILES, 1], F32)
+        nc.gpsimd.iota(
+            pos[:], pattern=[[P, TILES], [1, 1]], base=0, channel_multiplier=1, allow_small_or_imprecise_dtypes=True
+        )
+        zero(nc.vector, x_plane)
+        zero(nc.gpsimd, qa_plane)
+        zero(nc.gpsimd, qb_plane)
+        zero(nc.gpsimd, k_plane)
+
+        load_codes(x_codes, x_words, 0, 1, 0, TOKENS)
+        load_codes(qa_codes, Wq_words, 0, 1, 0, BLOCK)
+        load_scales(x_plane, x_scales, 0, TOKENS)
+        load_scales(qa_plane, Wq_scales, 0, BLOCK)
+        for g0, g1 in ((1, 2), (2, 4), (4, 6)):
+            load_codes(x_codes, x_words, g0, g1, 0, TOKENS)
+            load_codes(qa_codes, Wq_words, g0, g1, 0, BLOCK)
+        load_scales(qb_plane, Wq_scales, BLOCK, 3 * BLOCK)
+        for g in range(0, PASSES, 2):
+            load_codes(qb_codes, Wq_words, g, g + 2, BLOCK, 3 * BLOCK)
+        load_scales(k_plane, Wk_scales, 0, 3 * BLOCK)
+        for g in range(0, PASSES, 2):
+            load_codes(k_codes, Wk_words, g, g + 2, 0, 3 * BLOCK)
+
+        turns = keep.tile([P, TILES, 2, HALF], F32)
+        whole = keep.tile([P, TILES, 2, HALF], I32)
+        frac = keep.tile([P, TILES, 2, HALF], F32)
+        ratio = ROPE_BASE ** (-1.0 / HALF)
+        nc.vector.tensor_scalar(turns[:, :, 1, 0:1], pos[:], 1.0 / (2.0 * math.pi), 0.0, MULT, ADD)
+        for m in (1, 2, 4, 8, 16):
+            nc.vector.tensor_scalar(turns[:, :, 1, m : 2 * m], turns[:, :, 1, 0:m], ratio**m, 0.0, MULT, ADD)
+        nc.vector.tensor_scalar(turns[:, :, 1, 32:48], turns[:, :, 1, 16:32], ratio**16, 0.0, MULT, ADD)
+        nc.vector.tensor_scalar(turns[:, :, 0, :], turns[:, :, 1, :], 1.0, 0.25, MULT, ADD)
+        nc.vector.tensor_copy(out=whole[:], in_=turns[:])
+        nc.vector.tensor_tensor(frac[:], turns[:], whole[:], SUB)
+
+        cos_t = keep.tile([P, TILES, PERIODS * HEAD], F32)
+        sin_t = keep.tile([P, TILES, PERIODS * HEAD], F32)
+        for i in range(TILES):
+            nc.scalar.activation(
+                cos_t[:, i, :].rearrange("p (r j) -> p r j", j=HALF),
+                frac[:, i, 0:1, :].to_broadcast([P, 2 * PERIODS, HALF]),
+                SIN,
+                scale=2.0 * math.pi,
+            )
+            halves = sin_t[:, i, :].rearrange("p (r s j) -> p r s j", s=2, j=HALF)
+            for s in range(2):
+                nc.scalar.activation(
+                    halves[:, :, s, :],
+                    frac[:, i, 1:2, :].to_broadcast([P, PERIODS, HALF]),
+                    SIN,
+                    scale=(1 - 2 * s) * 2.0 * math.pi,
+                )
+
+        operands = []
+        operands.append((qa_codes, qa_plane, 0))
+        operands.append((qb_codes, qb_plane, 0))
+        operands.append((qb_codes, qb_plane, BLOCK))
+        for b in range(BLOCKS):
+            operands.append((k_codes, k_plane, b * BLOCK))
+
+        def mx_pass(acc, i, g, n, off=0, width=BLOCK):
+            codes, plane, c0 = operands[n]
+            c0 += off
+            nc.tensor.matmul_mx(
+                out=acc[:, 0:width],
+                lhsT=x_codes[:, g, 256 * i : 256 * i + 256].bitcast(FP4X4),
+                lhsT_scale=x_plane[:, g, P * i : P * i + P],
+                rhs=codes[:, g, 2 * c0 : 2 * c0 + 2 * width].bitcast(FP4X4),
+                rhs_scale=plane[:, g, c0 : c0 + width],
+                start=(g == 0),
+                stop=(g == PASSES - 1),
+            )
+
+        rows = {}
+        outs = (out_0, out_1)
+
+        def epilogue(acc, i, n, off=0, width=BLOCK, adder=nc.gpsimd):
+            w, b = divmod(n, BLOCKS)
+            if b == 0:
+                by_cos = prod.tile([P, OUT_FEATURES], F32, name="by_cos")
+                by_sin = prod.tile([P, OUT_FEATURES], F32, name="by_sin")
+                rows[w, i] = (by_cos, by_sin)
+            by_cos, by_sin = rows[w, i]
+            c0 = b * BLOCK + off
+            c1 = c0 + width
+            phase = c0 % HEAD
+            nc.vector.tensor_tensor(by_cos[:, c0:c1], acc[:, 0:width], cos_t[:, i, phase : phase + width], MULT)
+            nc.vector.tensor_tensor(by_sin[:, c0:c1], acc[:, 0:width], sin_t[:, i, phase : phase + width], MULT)
+            h0 = c0 // HEAD
+            h1 = c1 // HEAD
+            n_heads = h1 - h0
+            y = res.tile([P, 6, 2, HALF], F32, name="y")
+            c = by_cos[:, h0 * HEAD : h1 * HEAD].rearrange("p (h s j) -> p h s j", s=2, j=HALF)
+            d = by_sin[:, h0 * HEAD : h1 * HEAD].rearrange("p (h s j) -> p h s j", s=2, j=HALF)
+            adder.tensor_tensor(y[:, 0:n_heads, :, :], c, d[:, :, ::-1, :], ADD)
+            nc.sync.dma_start(
+                out=outs[w][0, h0:h1, P * i : P * i + P, :].rearrange("h p c -> p h c"),
+                in_=y[:, 0:n_heads, :, :].rearrange("p h s j -> p h (s j)"),
+            )
+
+        accs = []
+        for i in range(TILES):
+            acc = psum.tile([P, BLOCK], F32, name="acc")
+            accs.append(acc)
+        for g in range(PASSES):
+            for i in range(TILES):
+                mx_pass(accs[i], i, g, 0)
+        for i in range(TILES):
+            epilogue(accs[i], i, 0)
+        for n in range(1, 2 * BLOCKS):
+            for i in range(TILES):
+                if n == 2 * BLOCKS - 1 and i == TILES - 1:
+                    for off, width in ((0, 256), (256, 128), (384, 128)):
+                        acc = psum.tile([P, BLOCK], F32, name="acc")
+                        for g in range(PASSES):
+                            mx_pass(acc, i, g, n, off, width)
+                        epilogue(acc, i, n, off, width, nc.vector)
+                    continue
+                acc = psum.tile([P, BLOCK], F32, name="acc")
+                for g in range(PASSES):
+                    mx_pass(acc, i, g, n)
+                epilogue(acc, i, n)

@@ -4,6 +4,7 @@ from contextlib import ExitStack
 import concourse.mybir as mybir
 
 F32 = mybir.dt.float32
+BF16 = mybir.dt.bfloat16
 I32 = mybir.dt.int32
 U8 = mybir.dt.uint8
 FP4X4 = mybir.dt.float4_e2m1fn_x4
@@ -43,8 +44,10 @@ def tile_multiheadattention_pa_kernel(
         x_plane = keep.tile([P, PASSES, TOKENS], U8, align_bytes=64)
         qa_codes = keep.tile([P, PASSES, 2 * BLOCK], U8, align_bytes=64)
         qa_plane = keep.tile([P, PASSES, BLOCK], U8, align_bytes=64)
-        qb_codes = keep.tile([P, PASSES, 4 * BLOCK], U8, align_bytes=64)
-        qb_plane = keep.tile([P, PASSES, 2 * BLOCK], U8, align_bytes=64)
+        qb_codes = keep.tile([P, PASSES, 2 * BLOCK], U8, align_bytes=64)
+        qb_plane = keep.tile([P, PASSES, BLOCK], U8, align_bytes=64)
+        qc_codes = keep.tile([P, PASSES, 2 * BLOCK], U8, align_bytes=64)
+        qc_plane = keep.tile([P, PASSES, BLOCK], U8, align_bytes=64)
         k_codes = keep.tile([P, PASSES, 6 * BLOCK], U8, align_bytes=64)
         k_plane = keep.tile([P, PASSES, 3 * BLOCK], U8, align_bytes=64)
 
@@ -58,19 +61,22 @@ def tile_multiheadattention_pa_kernel(
             )
 
         def load_scales(plane, scales, c0, c1):
-            for q in range(4):
+            for r in range(4):
                 nc.sync.dma_start(
-                    out=plane[32 * q : 32 * q + 4, :, :].bitcast(I32),
-                    in_=scales[:, 4 * q : 4 * q + 4, c0:c1].rearrange("g r n -> r g n").bitcast(I32),
+                    out=plane[r:P:32, :, :].bitcast(I32),
+                    in_=scales[:, r:16:4, c0:c1].rearrange("g q n -> q g n").bitcast(I32),
                 )
 
         pos = keep.tile([P, TILES, 1], F32)
         nc.gpsimd.iota(
             pos[:], pattern=[[P, TILES], [1, 1]], base=0, channel_multiplier=1, allow_small_or_imprecise_dtypes=True
         )
+        idle = keep.tile([P, BLOCK], BF16)
+        nc.vector.memset(idle[:], 0.0)
         zero(nc.vector, x_plane)
         zero(nc.gpsimd, qa_plane)
         zero(nc.gpsimd, qb_plane)
+        zero(nc.gpsimd, qc_plane)
         zero(nc.gpsimd, k_plane)
 
         load_codes(x_codes, x_words, 0, 1, 0, TOKENS)
@@ -80,9 +86,12 @@ def tile_multiheadattention_pa_kernel(
         for g0, g1 in ((1, 2), (2, 4), (4, 6)):
             load_codes(x_codes, x_words, g0, g1, 0, TOKENS)
             load_codes(qa_codes, Wq_words, g0, g1, 0, BLOCK)
-        load_scales(qb_plane, Wq_scales, BLOCK, 3 * BLOCK)
-        for g in range(0, PASSES, 2):
-            load_codes(qb_codes, Wq_words, g, g + 2, BLOCK, 3 * BLOCK)
+        load_scales(qb_plane, Wq_scales, BLOCK, 2 * BLOCK)
+        for g in range(0, PASSES, 3):
+            load_codes(qb_codes, Wq_words, g, g + 3, BLOCK, 2 * BLOCK)
+        load_scales(qc_plane, Wq_scales, 2 * BLOCK, 3 * BLOCK)
+        for g in range(0, PASSES, 3):
+            load_codes(qc_codes, Wq_words, g, g + 3, 2 * BLOCK, 3 * BLOCK)
         load_scales(k_plane, Wk_scales, 0, 3 * BLOCK)
         for g in range(0, PASSES, 2):
             load_codes(k_codes, Wk_words, g, g + 2, 0, 3 * BLOCK)
@@ -120,7 +129,7 @@ def tile_multiheadattention_pa_kernel(
         operands = []
         operands.append((qa_codes, qa_plane, 0))
         operands.append((qb_codes, qb_plane, 0))
-        operands.append((qb_codes, qb_plane, BLOCK))
+        operands.append((qc_codes, qc_plane, 0))
         for b in range(BLOCKS):
             operands.append((k_codes, k_plane, b * BLOCK))
 
@@ -140,7 +149,7 @@ def tile_multiheadattention_pa_kernel(
         rows = {}
         outs = (out_0, out_1)
 
-        def epilogue(acc, i, n, off=0, width=BLOCK, adder=nc.gpsimd):
+        def products(acc, i, n, off=0, width=BLOCK):
             w, b = divmod(n, BLOCKS)
             if b == 0:
                 by_cos = prod.tile([P, OUT_FEATURES], F32, name="by_cos")
@@ -148,21 +157,26 @@ def tile_multiheadattention_pa_kernel(
                 rows[w, i] = (by_cos, by_sin)
             by_cos, by_sin = rows[w, i]
             c0 = b * BLOCK + off
-            c1 = c0 + width
             phase = c0 % HEAD
-            nc.vector.tensor_tensor(by_cos[:, c0:c1], acc[:, 0:width], cos_t[:, i, phase : phase + width], MULT)
-            nc.vector.tensor_tensor(by_sin[:, c0:c1], acc[:, 0:width], sin_t[:, i, phase : phase + width], MULT)
-            h0 = c0 // HEAD
-            h1 = c1 // HEAD
-            n_heads = h1 - h0
+            for out, table in ((by_cos, cos_t), (by_sin, sin_t)):
+                nc.vector.tensor_tensor(
+                    out[:, c0 : c0 + width], acc[:, 0:width], table[:, i, phase : phase + width], MULT
+                )
+
+        def heads(engine, w, i, h0, h1):
+            by_cos, by_sin = rows[w, i]
             y = res.tile([P, 6, 2, HALF], F32, name="y")
             c = by_cos[:, h0 * HEAD : h1 * HEAD].rearrange("p (h s j) -> p h s j", s=2, j=HALF)
             d = by_sin[:, h0 * HEAD : h1 * HEAD].rearrange("p (h s j) -> p h s j", s=2, j=HALF)
-            adder.tensor_tensor(y[:, 0:n_heads, :, :], c, d[:, :, ::-1, :], ADD)
+            engine.tensor_tensor(y[:, 0 : h1 - h0, :, :], c, d[:, :, ::-1, :], ADD)
             nc.sync.dma_start(
                 out=outs[w][0, h0:h1, P * i : P * i + P, :].rearrange("h p c -> p h c"),
-                in_=y[:, 0:n_heads, :, :].rearrange("p h s j -> p h (s j)"),
+                in_=y[:, 0 : h1 - h0, :, :].rearrange("p h s j -> p h (s j)"),
             )
+
+        warm = psum.tile([P, BLOCK], F32, name="acc")
+        for t in range(10):
+            nc.tensor.matmul(warm[:], lhsT=idle[:, 0:P], rhs=idle[:], start=True, stop=True)
 
         accs = []
         for i in range(TILES):
@@ -172,17 +186,30 @@ def tile_multiheadattention_pa_kernel(
             for i in range(TILES):
                 mx_pass(accs[i], i, g, 0)
         for i in range(TILES):
-            epilogue(accs[i], i, 0)
+            products(accs[i], i, 0)
+            heads(nc.gpsimd, 0, i, 0, 5)
+        last = 2 * BLOCKS - 1
         for n in range(1, 2 * BLOCKS):
+            w, b = divmod(n, BLOCKS)
             for i in range(TILES):
-                if n == 2 * BLOCKS - 1 and i == TILES - 1:
-                    for off, width in ((0, 256), (256, 128), (384, 128)):
-                        acc = psum.tile([P, BLOCK], F32, name="acc")
-                        for g in range(PASSES):
-                            mx_pass(acc, i, g, n, off, width)
-                        epilogue(acc, i, n, off, width, nc.vector)
-                    continue
-                acc = psum.tile([P, BLOCK], F32, name="acc")
-                for g in range(PASSES):
-                    mx_pass(acc, i, g, n)
-                epilogue(acc, i, n)
+                pieces = ((0, BLOCK),)
+                if n == last and i == TILES - 2:
+                    pieces = ((0, 256), (256, 256))
+                if n == last and i == TILES - 1:
+                    pieces = ((0, 256), (256, 128), (384, 128))
+                for off, width in pieces:
+                    acc = psum.tile([P, BLOCK], F32, name="acc")
+                    for g in range(PASSES):
+                        mx_pass(acc, i, g, n, off, width)
+                    products(acc, i, n, off, width)
+                    if n == last and i >= TILES - 2 and off == 0:
+                        heads(nc.gpsimd, w, i, 10, 13)
+                    if off + width == BLOCK:
+                        if n == last and i == TILES - 1:
+                            heads(nc.vector, w, i, 13, 16)
+                        elif (n, i) in ((last - 1, TILES - 2), (last, 0)):
+                            heads(nc.vector, w, i, b * BLOCK // HEAD, (b + 1) * BLOCK // HEAD)
+                        elif n == last and i == TILES - 2:
+                            heads(nc.gpsimd, w, i, 13, 16)
+                        else:
+                            heads(nc.gpsimd, w, i, b * BLOCK // HEAD, (b + 1) * BLOCK // HEAD)

@@ -178,38 +178,48 @@ def tile_multiheadattention_pa_kernel(
         for t in range(10):
             nc.tensor.matmul(warm[:], lhsT=idle[:, 0:P], rhs=idle[:], start=True, stop=True)
 
+        last = 2 * BLOCKS - 1
+        on_vector = (1, 4, 6, 9, 11, 14, 16, 19, 21)
+        waiting = []
+
+        def finish(i, n, pieces):
+            w, b = divmod(n, BLOCKS)
+            for acc, off, width in pieces:
+                products(acc, i, n, off, width)
+                while waiting:
+                    heads(nc.vector, *waiting.pop())
+                if off + width < BLOCK:
+                    if off == 0:
+                        heads(nc.gpsimd, w, i, 10, 13)
+                elif n == last and i == TILES - 1:
+                    waiting.append((w, i, 13, 16))
+                elif n == last and i == TILES - 2:
+                    heads(nc.gpsimd, w, i, 13, 16)
+                elif TILES * n + i in on_vector:
+                    waiting.append((w, i, b * BLOCK // HEAD, (b + 1) * BLOCK // HEAD))
+                else:
+                    heads(nc.gpsimd, w, i, b * BLOCK // HEAD, (b + 1) * BLOCK // HEAD)
+
         accs = []
-        for i in range(TILES):
+        for i in range(TILES - 1):
             acc = psum.tile([P, BLOCK], F32, name="acc")
             accs.append(acc)
         for g in range(PASSES):
-            for i in range(TILES):
+            for i in range(TILES - 1):
                 mx_pass(accs[i], i, g, 0)
-        for i in range(TILES):
-            products(accs[i], i, 0)
-            heads(nc.gpsimd, 0, i, 0, 5)
-        last = 2 * BLOCKS - 1
-        for n in range(1, 2 * BLOCKS):
-            w, b = divmod(n, BLOCKS)
-            for i in range(TILES):
-                pieces = ((0, BLOCK),)
-                if n == last and i == TILES - 2:
-                    pieces = ((0, 256), (256, 256))
-                if n == last and i == TILES - 1:
-                    pieces = ((0, 256), (256, 128), (384, 128))
-                for off, width in pieces:
-                    acc = psum.tile([P, BLOCK], F32, name="acc")
-                    for g in range(PASSES):
-                        mx_pass(acc, i, g, n, off, width)
-                    products(acc, i, n, off, width)
-                    if n == last and i >= TILES - 2 and off == 0:
-                        heads(nc.gpsimd, w, i, 10, 13)
-                    if off + width == BLOCK:
-                        if n == last and i == TILES - 1:
-                            heads(nc.vector, w, i, 13, 16)
-                        elif (n, i) in ((last - 1, TILES - 2), (last, 0)):
-                            heads(nc.vector, w, i, b * BLOCK // HEAD, (b + 1) * BLOCK // HEAD)
-                        elif n == last and i == TILES - 2:
-                            heads(nc.gpsimd, w, i, 13, 16)
-                        else:
-                            heads(nc.gpsimd, w, i, b * BLOCK // HEAD, (b + 1) * BLOCK // HEAD)
+        for i in range(TILES - 1):
+            finish(i, 0, ((accs[i], 0, BLOCK),))
+        for m in range(TILES - 1, 2 * BLOCKS * TILES):
+            n, i = divmod(m, TILES)
+            cuts = ((0, BLOCK),)
+            if n == last and i == TILES - 2:
+                cuts = ((0, 256), (256, 256))
+            if n == last and i == TILES - 1:
+                cuts = ((0, 256), (256, 128), (384, 128))
+            for off, width in cuts:
+                acc = psum.tile([P, BLOCK], F32, name="acc")
+                for g in range(PASSES):
+                    mx_pass(acc, i, g, n, off, width)
+                finish(i, n, ((acc, off, width),))
+        while waiting:
+            heads(nc.vector, *waiting.pop())

@@ -72,7 +72,7 @@ def tile_multiheadattention_pa_kernel(
             pos[:], pattern=[[P, TILES], [1, 1]], base=0, channel_multiplier=1, allow_small_or_imprecise_dtypes=True
         )
         idle = keep.tile([P, BLOCK], BF16)
-        nc.vector.memset(idle[:], 0.0)
+        nc.vector.memset(idle[:].bitcast(F32), 0.0)
         zero(nc.vector, x_plane)
         zero(nc.gpsimd, qa_plane)
         zero(nc.gpsimd, qb_plane)
@@ -108,16 +108,15 @@ def tile_multiheadattention_pa_kernel(
         nc.vector.tensor_copy(out=whole[:], in_=turns[:])
         nc.vector.tensor_tensor(frac[:], turns[:], whole[:], SUB)
 
-        cos_t = keep.tile([P, TILES, PERIODS * HEAD], F32)
-        sin_t = keep.tile([P, TILES, PERIODS * HEAD], F32)
+        tables = keep.tile([P, TILES, 2, PERIODS * HEAD], F32)
         for i in range(TILES):
             nc.scalar.activation(
-                cos_t[:, i, :].rearrange("p (r j) -> p r j", j=HALF),
+                tables[:, i, 0, :].rearrange("p (r j) -> p r j", j=HALF),
                 frac[:, i, 0:1, :].to_broadcast([P, 2 * PERIODS, HALF]),
                 SIN,
                 scale=2.0 * math.pi,
             )
-            halves = sin_t[:, i, :].rearrange("p (r s j) -> p r s j", s=2, j=HALF)
+            halves = tables[:, i, 1, :].rearrange("p (r s j) -> p r s j", s=2, j=HALF)
             for s in range(2):
                 nc.scalar.activation(
                     halves[:, :, s, :],
@@ -137,7 +136,7 @@ def tile_multiheadattention_pa_kernel(
             codes, plane, c0 = operands[n]
             c0 += off
             nc.tensor.matmul_mx(
-                out=acc[:, 0:width],
+                out=acc[:, 0, 0:width],
                 lhsT=x_codes[:, g, 256 * i : 256 * i + 256].bitcast(FP4X4),
                 lhsT_scale=x_plane[:, g, P * i : P * i + P],
                 rhs=codes[:, g, 2 * c0 : 2 * c0 + 2 * width].bitcast(FP4X4),
@@ -151,75 +150,72 @@ def tile_multiheadattention_pa_kernel(
 
         def products(acc, i, n, off=0, width=BLOCK):
             w, b = divmod(n, BLOCKS)
-            if b == 0:
-                by_cos = prod.tile([P, OUT_FEATURES], F32, name="by_cos")
-                by_sin = prod.tile([P, OUT_FEATURES], F32, name="by_sin")
-                rows[w, i] = (by_cos, by_sin)
-            by_cos, by_sin = rows[w, i]
+            if (w, i) not in rows:
+                both = prod.tile([P, 2, OUT_FEATURES], F32, name="both")
+                rows[w, i] = both
             c0 = b * BLOCK + off
             phase = c0 % HEAD
-            for out, table in ((by_cos, cos_t), (by_sin, sin_t)):
-                nc.vector.tensor_tensor(
-                    out[:, c0 : c0 + width], acc[:, 0:width], table[:, i, phase : phase + width], MULT
-                )
+            nc.vector.tensor_tensor(
+                rows[w, i][:, :, c0 : c0 + width],
+                acc[:, :, 0:width].to_broadcast([P, 2, width]),
+                tables[:, i, :, phase : phase + width],
+                MULT,
+            )
 
         def heads(engine, w, i, h0, h1):
-            by_cos, by_sin = rows[w, i]
             y = res.tile([P, 6, 2, HALF], F32, name="y")
-            c = by_cos[:, h0 * HEAD : h1 * HEAD].rearrange("p (h s j) -> p h s j", s=2, j=HALF)
-            d = by_sin[:, h0 * HEAD : h1 * HEAD].rearrange("p (h s j) -> p h s j", s=2, j=HALF)
+            span = rows[w, i][:, :, h0 * HEAD : h1 * HEAD]
+            c = span[:, 0, :].rearrange("p (h s j) -> p h s j", s=2, j=HALF)
+            d = span[:, 1, :].rearrange("p (h s j) -> p h s j", s=2, j=HALF)
             engine.tensor_tensor(y[:, 0 : h1 - h0, :, :], c, d[:, :, ::-1, :], ADD)
             nc.sync.dma_start(
                 out=outs[w][0, h0:h1, P * i : P * i + P, :].rearrange("h p c -> p h c"),
                 in_=y[:, 0 : h1 - h0, :, :].rearrange("p h s j -> p h (s j)"),
             )
 
-        warm = psum.tile([P, BLOCK], F32, name="acc")
-        for t in range(10):
-            nc.tensor.matmul(warm[:], lhsT=idle[:, 0:P], rhs=idle[:], start=True, stop=True)
+        def bank():
+            acc = psum.tile([P, 1, BLOCK], F32, name="acc")
+            return acc
+
+        warm = bank()
+        for t in range(11):
+            nc.tensor.matmul(warm[:, 0, :], lhsT=idle[:, 0:P], rhs=idle[:], start=True, stop=True)
 
         last = 2 * BLOCKS - 1
-        on_vector = (1, 4, 6, 9, 11, 14, 16, 19, 21)
-        waiting = []
+        late = []
 
-        def finish(i, n, pieces):
-            w, b = divmod(n, BLOCKS)
-            for acc, off, width in pieces:
-                products(acc, i, n, off, width)
-                while waiting:
-                    heads(nc.vector, *waiting.pop())
-                if off + width < BLOCK:
-                    if off == 0:
-                        heads(nc.gpsimd, w, i, 10, 13)
-                elif n == last and i == TILES - 1:
-                    waiting.append((w, i, 13, 16))
-                elif n == last and i == TILES - 2:
-                    heads(nc.gpsimd, w, i, 13, 16)
-                elif TILES * n + i in on_vector:
-                    waiting.append((w, i, b * BLOCK // HEAD, (b + 1) * BLOCK // HEAD))
-                else:
-                    heads(nc.gpsimd, w, i, b * BLOCK // HEAD, (b + 1) * BLOCK // HEAD)
+        def add_late():
+            while late:
+                heads(nc.vector, *late.pop(0))
 
-        accs = []
-        for i in range(TILES - 1):
-            acc = psum.tile([P, BLOCK], F32, name="acc")
-            accs.append(acc)
+        def add(m, h0, h1):
+            n, i = divmod(m, TILES)
+            if m % 3 == 2 or m >= 22:
+                late.append((n // BLOCKS, i, h0, h1))
+            else:
+                heads(nc.gpsimd, n // BLOCKS, i, h0, h1)
+
+        accs = [bank() for i in range(TILES - 1)]
         for g in range(PASSES):
             for i in range(TILES - 1):
                 mx_pass(accs[i], i, g, 0)
         for i in range(TILES - 1):
-            finish(i, 0, ((accs[i], 0, BLOCK),))
+            products(accs[i], i, 0)
+            add_late()
+            add(i, 0, 5)
         for m in range(TILES - 1, 2 * BLOCKS * TILES):
             n, i = divmod(m, TILES)
-            cuts = ((0, BLOCK),)
-            if n == last and i == TILES - 2:
-                cuts = ((0, 256), (256, 256))
-            if n == last and i == TILES - 1:
-                cuts = ((0, 256), (256, 128), (384, 128))
-            for off, width in cuts:
-                acc = psum.tile([P, BLOCK], F32, name="acc")
+            b = n % BLOCKS
+            width = BLOCK if n < last else BLOCK // 2
+            for off in range(0, BLOCK, width):
+                acc = bank()
                 for g in range(PASSES):
                     mx_pass(acc, i, g, n, off, width)
-                finish(i, n, ((acc, off, width),))
-        while waiting:
-            heads(nc.vector, *waiting.pop())
+                products(acc, i, n, off, width)
+                add_late()
+                if m == 23:
+                    h = b * BLOCK // HEAD
+                    add(m, (h, 13)[off > 0], (13, 16)[off > 0])
+            if m < 23:
+                add(m, b * BLOCK // HEAD, (b + 1) * BLOCK // HEAD)
+        add_late()

import math
from contextlib import ExitStack

import concourse.mybir as mybir

F32 = mybir.dt.float32
BF16 = mybir.dt.bfloat16
I32 = mybir.dt.int32
U8 = mybir.dt.uint8
FP4X4 = mybir.dt.float4_e2m1fn_x4
ADD = mybir.AluOpType.add
SUB = mybir.AluOpType.subtract
MULT = mybir.AluOpType.mult
SIN = mybir.ActivationFunctionType.Sin

P = 128
TOKENS = 512
FEATURES = 3072
OUT_FEATURES = 1536
HEADS = 16
HEAD = 96
HALF = HEAD // 2
PASSES = FEATURES // 512
TILES = TOKENS // P
BLOCK = 512
BLOCKS = OUT_FEATURES // BLOCK
ROPE_BASE = 10000.0
PERIODS = 6
FLOPS = 2 * TOKENS * FEATURES * 2 * OUT_FEATURES


def tile_multiheadattention_pa_kernel(
    tc, x_words, x_scales, Wq_words, Wq_scales, Wk_words, Wk_scales, out_0, out_1
):
    nc = tc.nc
    with ExitStack() as ctx:
        ctx.enter_context(tc.manual_schedule())
        keep = ctx.enter_context(tc.tile_pool(name="keep", bufs=1))
        prod = ctx.enter_context(tc.tile_pool(name="prod", bufs=8))
        res = ctx.enter_context(tc.tile_pool(name="res", bufs=6))
        psum = ctx.enter_context(tc.psum_pool(name="psum", bufs=8))

        x_codes = keep.tile([P, PASSES, 2 * TOKENS], U8, align_bytes=64)
        x_plane = keep.tile([P, PASSES, TOKENS], U8, align_bytes=64)
        qa_codes = keep.tile([P, PASSES, 2 * BLOCK], U8, align_bytes=64)
        qa_plane = keep.tile([P, PASSES, BLOCK], U8, align_bytes=64)
        qb_codes = keep.tile([P, PASSES, 2 * BLOCK], U8, align_bytes=64)
        qb_plane = keep.tile([P, PASSES, BLOCK], U8, align_bytes=64)
        qc_codes = keep.tile([P, PASSES, 2 * BLOCK], U8, align_bytes=64)
        qc_plane = keep.tile([P, PASSES, BLOCK], U8, align_bytes=64)
        k_codes = keep.tile([P, PASSES, 6 * BLOCK], U8, align_bytes=64)
        k_plane = keep.tile([P, PASSES, 3 * BLOCK], U8, align_bytes=64)

        def zero(engine, plane):
            engine.memset(plane[:].rearrange("p g n -> p (g n)").bitcast(I32), 0)

        def load_codes(tile, words, g0, g1, c0, c1):
            nc.sync.dma_start(
                out=tile[:, g0:g1, :].bitcast(I32),
                in_=words[g0:g1, :, 2 * c0 : 2 * c1].rearrange("g p n -> p g n").bitcast(I32),
            )

        def load_scales(plane, scales, c0, c1):
            for r in range(4):
                nc.sync.dma_start(
                    out=plane[r:P:32, :, :].bitcast(I32),
                    in_=scales[:, r:16:4, c0:c1].rearrange("g q n -> q g n").bitcast(I32),
                )

        pos = keep.tile([P, TILES, 1], F32)
        nc.gpsimd.iota(
            pos[:], pattern=[[P, TILES], [1, 1]], base=0, channel_multiplier=1, allow_small_or_imprecise_dtypes=True
        )
        idle = keep.tile([P, BLOCK], BF16)
        nc.vector.memset(idle[:].bitcast(F32), 0.0)
        zero(nc.vector, x_plane)
        zero(nc.gpsimd, qa_plane)
        zero(nc.gpsimd, qb_plane)
        zero(nc.gpsimd, qc_plane)
        zero(nc.gpsimd, k_plane)

        load_codes(x_codes, x_words, 0, 1, 0, TOKENS)
        load_codes(qa_codes, Wq_words, 0, 1, 0, BLOCK)
        load_scales(x_plane, x_scales, 0, TOKENS)
        load_scales(qa_plane, Wq_scales, 0, BLOCK)
        for g0, g1 in ((1, 2), (2, 4), (4, 6)):
            load_codes(x_codes, x_words, g0, g1, 0, TOKENS)
            load_codes(qa_codes, Wq_words, g0, g1, 0, BLOCK)
        load_scales(qb_plane, Wq_scales, BLOCK, 2 * BLOCK)
        for g in range(0, PASSES, 3):
            load_codes(qb_codes, Wq_words, g, g + 3, BLOCK, 2 * BLOCK)
        load_scales(qc_plane, Wq_scales, 2 * BLOCK, 3 * BLOCK)
        for g in range(0, PASSES, 3):
            load_codes(qc_codes, Wq_words, g, g + 3, 2 * BLOCK, 3 * BLOCK)
        load_scales(k_plane, Wk_scales, 0, 3 * BLOCK)
        for g in range(0, PASSES, 2):
            load_codes(k_codes, Wk_words, g, g + 2, 0, 3 * BLOCK)

        turns = keep.tile([P, TILES, 2, HALF], F32)
        whole = keep.tile([P, TILES, 2, HALF], I32)
        frac = keep.tile([P, TILES, 2, HALF], F32)
        ratio = ROPE_BASE ** (-1.0 / HALF)
        nc.vector.tensor_scalar(turns[:, :, 1, 0:1], pos[:], 1.0 / (2.0 * math.pi), 0.0, MULT, ADD)
        for m in (1, 2, 4, 8, 16):
            nc.vector.tensor_scalar(turns[:, :, 1, m : 2 * m], turns[:, :, 1, 0:m], ratio**m, 0.0, MULT, ADD)
        nc.vector.tensor_scalar(turns[:, :, 1, 32:48], turns[:, :, 1, 16:32], ratio**16, 0.0, MULT, ADD)
        nc.vector.tensor_scalar(turns[:, :, 0, :], turns[:, :, 1, :], 1.0, 0.25, MULT, ADD)
        nc.vector.tensor_copy(out=whole[:], in_=turns[:])
        nc.vector.tensor_tensor(frac[:], turns[:], whole[:], SUB)

        tables = keep.tile([P, TILES, 2, PERIODS * HEAD], F32)
        for i in range(TILES):
            nc.scalar.activation(
                tables[:, i, 0, :].rearrange("p (r j) -> p r j", j=HALF),
                frac[:, i, 0:1, :].to_broadcast([P, 2 * PERIODS, HALF]),
                SIN,
                scale=2.0 * math.pi,
            )
            halves = tables[:, i, 1, :].rearrange("p (r s j) -> p r s j", s=2, j=HALF)
            for s in range(2):
                nc.scalar.activation(
                    halves[:, :, s, :],
                    frac[:, i, 1:2, :].to_broadcast([P, PERIODS, HALF]),
                    SIN,
                    scale=(1 - 2 * s) * 2.0 * math.pi,
                )

        operands = []
        operands.append((qa_codes, qa_plane, 0))
        operands.append((qb_codes, qb_plane, 0))
        operands.append((qc_codes, qc_plane, 0))
        for b in range(BLOCKS):
            operands.append((k_codes, k_plane, b * BLOCK))

        def mx_pass(acc, i, g, n, off=0, width=BLOCK):
            codes, plane, c0 = operands[n]
            c0 += off
            nc.tensor.matmul_mx(
                out=acc[:, 0, 0:width],
                lhsT=x_codes[:, g, 256 * i : 256 * i + 256].bitcast(FP4X4),
                lhsT_scale=x_plane[:, g, P * i : P * i + P],
                rhs=codes[:, g, 2 * c0 : 2 * c0 + 2 * width].bitcast(FP4X4),
                rhs_scale=plane[:, g, c0 : c0 + width],
                start=(g == 0),
                stop=(g == PASSES - 1),
            )

        rows = {}
        outs = (out_0, out_1)

        def products(acc, i, n, off=0, width=BLOCK):
            w, b = divmod(n, BLOCKS)
            if (w, i) not in rows:
                both = prod.tile([P, 2, OUT_FEATURES], F32, name="both")
                rows[w, i] = both
            c0 = b * BLOCK + off
            phase = c0 % HEAD
            nc.vector.tensor_tensor(
                rows[w, i][:, :, c0 : c0 + width],
                acc[:, :, 0:width].to_broadcast([P, 2, width]),
                tables[:, i, :, phase : phase + width],
                MULT,
            )

        def heads(engine, w, i, h0, h1):
            y = res.tile([P, 6, 2, HALF], F32, name="y")
            span = rows[w, i][:, :, h0 * HEAD : h1 * HEAD]
            c = span[:, 0, :].rearrange("p (h s j) -> p h s j", s=2, j=HALF)
            d = span[:, 1, :].rearrange("p (h s j) -> p h s j", s=2, j=HALF)
            engine.tensor_tensor(y[:, 0 : h1 - h0, :, :], c, d[:, :, ::-1, :], ADD)
            nc.sync.dma_start(
                out=outs[w][0, h0:h1, P * i : P * i + P, :].rearrange("h p c -> p h c"),
                in_=y[:, 0 : h1 - h0, :, :].rearrange("p h s j -> p h (s j)"),
            )

        def bank():
            acc = psum.tile([P, 1, BLOCK], F32, name="acc")
            return acc

        warm = bank()
        for t in range(11):
            nc.tensor.matmul(warm[:, 0, :], lhsT=idle[:, 0:P], rhs=idle[:], start=True, stop=True)

        last = 2 * BLOCKS - 1
        late = []

        def add_late():
            while late:
                heads(nc.vector, *late.pop(0))

        def add(m, h0, h1):
            n, i = divmod(m, TILES)
            if m % 3 == 2 or m >= 22:
                late.append((n // BLOCKS, i, h0, h1))
            else:
                heads(nc.gpsimd, n // BLOCKS, i, h0, h1)

        accs = [bank() for i in range(TILES - 1)]
        for g in range(PASSES):
            for i in range(TILES - 1):
                mx_pass(accs[i], i, g, 0)
        for i in range(TILES - 1):
            products(accs[i], i, 0)
            add_late()
            add(i, 0, 5)
        for m in range(TILES - 1, 2 * BLOCKS * TILES):
            n, i = divmod(m, TILES)
            b = n % BLOCKS
            width = BLOCK if n < last else BLOCK // 2
            for off in range(0, BLOCK, width):
                acc = bank()
                for g in range(PASSES):
                    mx_pass(acc, i, g, n, off, width)
                products(acc, i, n, off, width)
                add_late()
                if m == 23:
                    h = b * BLOCK // HEAD
                    add(m, (h, 13)[off > 0], (13, 16)[off > 0])
            if m < 23:
                add(m, b * BLOCK // HEAD, (b + 1) * BLOCK // HEAD)
        add_late()
